import numpy as np
import ml_dtypes


def mxq(x, axis, fmt="e4m3"):
    dtype, down = {"e4m3": (ml_dtypes.float8_e4m3fn, 7), "e5m2": (ml_dtypes.float8_e5m2, 14)}[fmt]
    v = np.moveaxis(np.asarray(x, np.float32).astype(ml_dtypes.bfloat16).astype(np.float64), axis, -1)
    blocks = v.reshape(v.shape[:-1] + (-1, 32))
    amax = np.abs(blocks).max(-1, keepdims=True)
    byte = np.maximum(np.where(amax > 0, np.frexp(amax)[1] - 1 + 127, 0) - down, 1)
    scale = np.exp2(byte - 127.0)
    codes = (blocks / scale).astype(np.float32).astype(dtype).astype(np.float64)
    return np.moveaxis((codes * scale).reshape(v.shape), -1, axis)


WIDE = False


def mx_kscale(k):
    if not WIDE:
        return np.ones(k)
    levels = np.array([10, -10, 5, -5, 0])
    a = np.random.permutation(np.resize(levels, k // 512 * 4)).reshape(k // 512, 4)
    idx = np.arange(k)
    return np.exp2(a[idx // 512, idx % 128 // 32])


BF16 = ml_dtypes.bfloat16


def bf(x):
    return np.asarray(x, np.float32).astype(BF16)


def f64(x):
    return np.asarray(x).astype(np.float64)


E, T, G, C = 1408, 3, 3, 512


def silu(v):
    return v / (1.0 + np.exp(-v))


def setup_inputs():
    n = np.random.standard_normal
    s = mx_kscale(C)
    t = mx_kscale(G * C).reshape(G, C)
    r = np.sqrt(C)
    return {
        "edge": bf(n((E, C)) * s),
        "edge_nei_len": bf(n((E, T, C)) * s),
        "edge_nei_angle": bf(n((E, T, C)) * s),
        "Wk": bf(n((C, C)) / r / s[:, None] * t[0]),
        "bk": bf(n(C) * 0.2 * t[0]),
        "Wke": bf(n((T, C, C)) / r / s[:, None] * t[1]),
        "bke": bf(n((T, C)) * 0.2 * t[1]),
        "We": bf(n((C, C)) / r / s[:, None] * t[2]),
        "Wk1": bf(n((G * C, C)) / np.sqrt(G * C) / t.reshape(G * C, 1)),
        "bk1": bf(n(C) * 0.2),
    }


def reference(edge, edge_nei_len, edge_nei_angle, Wk, bk, Wke, bke, We, Wk1, bk1):
    kx = (mxq(f64(edge), 1, "e4m3") @ mxq(f64(Wk), 0, "e4m3")) + f64(bk)
    ky = (mxq(f64(edge_nei_len).transpose(1, 0, 2), 2, "e4m3") @ mxq(f64(Wke), 1, "e4m3")) + f64(bke)[:, None, :]
    ky = ky.transpose(1, 0, 2)
    exy = mxq(f64(edge_nei_angle), 2, "e4m3") @ mxq(f64(We), 0, "e4m3")
    w_x, w_y, w_e = f64(Wk1).reshape(G, C, C)
    pre = ((mxq(kx, 1, "e4m3") @ mxq(w_x, 0, "e4m3"))[:, None, :]
           + (mxq(ky, 2, "e4m3") @ mxq(w_y, 0, "e4m3"))
           + (mxq(exy, 2, "e4m3") @ mxq(w_e, 0, "e4m3"))
           + f64(bk1))
    return silu(pre)

@@ -1,0 +1,240 @@
+from contextlib import ExitStack
+
+import concourse.mybir as mybir
+from concourse.masks import make_identity
+
+F32 = mybir.dt.float32
+BF16 = mybir.dt.bfloat16
+U32 = mybir.dt.uint32
+U8 = mybir.dt.uint8
+FP8X4 = mybir.dt.float8_e4m3fn_x4
+ADD = mybir.AluOpType.add
+SILU = mybir.ActivationFunctionType.Silu
+
+P = 128
+PACK = 4
+E, T, C = 1408, 3, 512
+E_TILES = E // P
+ROW_TILES = 1 + 2 * T
+GROUPS = C // P
+WORDS = C // 2
+PSUM_BANKS = 8
+FIRST_LAYER = 2 + T
+BIASED = 1 + T
+WE = 1 + T
+UNITS = ((0, 1), (1, 2), (3, 2), (5, 2))
+
+FLOPS = 2 * 2 * ROW_TILES * E * C * C
+
+
+def tile_comformerconvedgelayer_pa_t_kernel(
+    tc, edge, edge_nei_len, edge_nei_angle, Wk, bk, Wke, bke, We, Wk1, bk1, out
+):
+    nc = tc.nc
+    with ExitStack() as stack:
+        def sbuf(name, bufs):
+            return stack.enter_context(tc.tile_pool(name=name, bufs=bufs))
+
+        const = sbuf("const", 1)
+        x_raw_pool = sbuf("x_raw", E_TILES)
+        w_raw_pool = sbuf("w_raw", FIRST_LAYER + T)
+        w_grouped_pool = sbuf("w_grouped", 3)
+        x_grouped_pool = sbuf("x_grouped", 3)
+        x_mx_pool = sbuf("x_mx", 3)
+        k_grouped_pool = sbuf("k_grouped", 3)
+        k_mx_pool = sbuf("k_mx", 3)
+        hidden_pool = sbuf("hidden", 6)
+        psum = stack.enter_context(tc.psum_pool(name="psum", bufs=PSUM_BANKS))
+
+        def load_x(i):
+            rows = slice(i * P, (i + 1) * P)
+            raw = x_raw_pool.tile([P, ROW_TILES * C], BF16, name="x_raw")
+            nc.sync.dma_start(out=raw[:, 0:C], in_=edge[rows, :])
+            nc.sync.dma_start(
+                out=raw[:, C : (1 + T) * C],
+                in_=edge_nei_len[rows].rearrange("e t c -> e (t c)"),
+            )
+            nc.sync.dma_start(
+                out=raw[:, (1 + T) * C : ROW_TILES * C],
+                in_=edge_nei_angle[rows].rearrange("e t c -> e (t c)"),
+            )
+            return raw
+
+        def place_in_x_raw(s):
+            t, is_angle = divmod(s - 1, 2)
+            return 0 if s == 0 else 1 + T * is_angle + t
+
+        def load_first_layer(w):
+            raw = w_raw_pool.tile([P, PACK, C], BF16, name="w_raw")
+            nc.sync.dma_start(
+                out=raw[:].rearrange("p (u e) c -> p u (e c)", u=2),
+                in_=w.rearrange("(u p e) c -> p u (e c)", u=2, e=2),
+            )
+            return raw
+
+        def load_second_layer(w):
+            raw = w_raw_pool.tile([P, PACK, C], BF16, name="w_raw")
+            nc.sync.dma_start(out=raw[:], in_=w.rearrange("(m p) c -> p m c", p=P))
+            return raw
+
+        x_raw = [load_x(0), load_x(1)]
+        w1_raw = [load_first_layer(w) for w in (Wk, Wke[0], Wke[1], Wke[2], We)]
+        x_raw.append(load_x(2))
+        w2_raw = [load_second_layer(Wk1[g * C : (g + 1) * C, :]) for g in range(T)]
+        for i in range(3, E_TILES):
+            x_raw.append(load_x(i))
+
+        ident = const.tile([P, P], F32, name="ident")
+        make_identity(nc, ident[:])
+
+        bias_rows = const.tile([P, P], BF16, name="bias_rows")
+        nc.vector.memset(bias_rows[:], 0.0)
+        nc.scalar.dma_start(out=bias_rows[0:GROUPS, :], in_=bk.rearrange("(m p) -> m p", p=P))
+        nc.scalar.dma_start(
+            out=bias_rows[GROUPS : BIASED * GROUPS, :],
+            in_=bke.rearrange("t (m p) -> (t m) p", p=P),
+        )
+        bias_rows_f32 = const.tile([P, P], F32, name="bias_rows_f32")
+        nc.vector.tensor_copy(out=bias_rows_f32[:], in_=bias_rows[:])
+        bias_bank = psum.tile([P, P], F32, name="bias_bank", tag="bank")
+        nc.tensor.transpose(bias_bank[:], bias_rows_f32[:], ident[:])
+        bias1 = const.tile([P, BIASED * GROUPS], F32, name="bias1")
+        nc.vector.tensor_copy(out=bias1[:], in_=bias_bank[:, 0 : BIASED * GROUPS])
+
+        bk1_row = const.tile([P, C], BF16, name="bk1_row")
+        nc.vector.memset(bk1_row[:], 0.0)
+        nc.scalar.dma_start(out=bk1_row[0:1, :], in_=bk1.rearrange("(o c) -> o c", o=1))
+        ones = const.tile([P, P], BF16, name="ones")
+        nc.vector.memset(ones[:], 1.0)
+        bk1_bank = psum.tile([P, C], F32, name="bk1_bank", tag="bank")
+        nc.tensor.matmul(out=bk1_bank[:], lhsT=ones[:], rhs=bk1_row[:], start=True, stop=True)
+        bk1_all = const.tile([P, C], F32, name="bk1_all")
+        nc.vector.tensor_copy(out=bk1_all[:], in_=bk1_bank[:])
+
+        w1_codes = const.tile([P, FIRST_LAYER * C], U32, name="w1_codes", align_bytes=64)
+        w1_scales = const.tile([P, FIRST_LAYER * C], U8, name="w1_scales", align_bytes=64)
+        w2_codes = const.tile([P, T * C], U32, name="w2_codes", align_bytes=64)
+        w2_scales = const.tile([P, T * C], U8, name="w2_scales", align_bytes=64)
+
+        def quantise_weights(raws, codes, scales):
+            grouped = []
+            for n in range(len(raws) + 1):
+                if n < len(raws):
+                    tile = w_grouped_pool.tile([P, C, PACK], BF16, name="w_grouped", align_bytes=64)
+                    copy = nc.vector.tensor_copy if n % 2 == 0 else nc.scalar.copy
+                    copy(
+                        out=tile[:].rearrange("p (c i) j -> p c j i", i=4),
+                        in_=raws[n][:].rearrange("p j (c i) -> p c j i", i=4),
+                    )
+                    grouped.append(tile)
+                if n > 0:
+                    cols = slice((n - 1) * C, n * C)
+                    nc.vector.quantize_mx(
+                        out=codes[:, cols].bitcast(FP8X4),
+                        scales=scales[:, cols],
+                        in_=grouped[n - 1][:].rearrange("p c j -> p (c j)"),
+                    )
+
+        x_grouped, x_mx, k_grouped, k_mx = {}, {}, {}, {}
+
+        def quantise_row_tiles(grouped, pool, name):
+            codes = pool.tile([P, ROW_TILES * P], U32, name=name + "_codes", align_bytes=64)
+            scales = pool.tile([P, ROW_TILES * P], U8, name=name + "_scales", align_bytes=64)
+            for first, count in UNITS:
+                words = slice(first * P, (first + count) * P)
+                nc.vector.quantize_mx(
+                    out=codes[:, words].bitcast(FP8X4),
+                    scales=scales[:, words],
+                    in_=grouped[:, first * C : (first + count) * C],
+                )
+            return codes, scales
+
+        def transpose_x(i):
+            grouped = x_grouped_pool.tile([P, ROW_TILES * C], BF16, name="x_grouped", align_bytes=64)
+            words_in = x_raw[i][:].bitcast(F32)
+            words_out = grouped[:].bitcast(F32)
+            for first, count in UNITS:
+                bank = psum.tile([P, 2, 2, P], F32, name="xt", tag="bank")
+                for j in range(count):
+                    for u in range(2):
+                        word = place_in_x_raw(first + j) * WORDS + u * P
+                        nc.tensor.transpose(bank[:, j, u, :], words_in[:, word : word + P], ident[:])
+                nc.scalar.copy(
+                    out=words_out[:, first * WORDS : (first + count) * WORDS].rearrange(
+                        "p (j r u) -> p j r u", j=count, u=2
+                    ),
+                    in_=bank[:, 0:count].rearrange("p j u r -> p j r u"),
+                )
+            x_grouped[i] = grouped
+
+        def project(i, s, w):
+            if s == 0:
+                k_grouped[i] = k_grouped_pool.tile(
+                    [P, ROW_TILES * C], BF16, name="k_grouped", align_bytes=64
+                )
+            codes, scales = x_mx[i]
+            rows = slice(s * P, (s + 1) * P)
+            bank = psum.tile([P, GROUPS, P], F32, name="k_bank", tag="bank")
+            for m in range(GROUPS):
+                channels = slice(w * C + m * P, w * C + (m + 1) * P)
+                nc.tensor.matmul_mx(
+                    out=bank[:, m, :],
+                    lhsT=w1_codes[:, channels].bitcast(FP8X4),
+                    lhsT_scale=w1_scales[:, channels],
+                    rhs=codes[:, rows].bitcast(FP8X4),
+                    rhs_scale=scales[:, rows],
+                    start=True,
+                    stop=True,
+                )
+            result = bank[:].rearrange("p m r -> p r m")
+            rounded = k_grouped[i][:, s * C : (s + 1) * C].rearrange("p (r m) -> p r m", m=GROUPS)
+            if w < BIASED:
+                bias = bias1[:, w * GROUPS : (w + 1) * GROUPS].unsqueeze(1).to_broadcast([P, P, GROUPS])
+                nc.vector.tensor_tensor(out=rounded, in0=result, in1=bias, op=ADD)
+            else:
+                nc.scalar.copy(out=rounded, in_=result)
+
+        def fuse(i, t):
+            codes, scales = k_mx[i]
+            acc = psum.tile([P, C], F32, name="acc", tag="bank")
+            for g, s in enumerate((0, 1 + 2 * t, 2 + 2 * t)):
+                rows = slice(s * P, (s + 1) * P)
+                w_cols = slice(g * C, (g + 1) * C)
+                nc.tensor.matmul_mx(
+                    out=acc[:],
+                    lhsT=codes[:, rows].bitcast(FP8X4),
+                    lhsT_scale=scales[:, rows],
+                    rhs=w2_codes[:, w_cols].bitcast(FP8X4),
+                    rhs_scale=w2_scales[:, w_cols],
+                    start=(g == 0),
+                    stop=(g == 2),
+                )
+            hidden = hidden_pool.tile([P, C], F32, name="hidden")
+            nc.vector.tensor_tensor(out=hidden[:], in0=acc[:], in1=bk1_all[:], op=ADD)
+            nc.scalar.activation(out=hidden[:], in_=hidden[:], func=SILU)
+            nc.sync.dma_start(out=out[i * P : (i + 1) * P, t, :], in_=hidden[:])
+
+        def step(i):
+            tiles = range(E_TILES)
+            if i + 3 in tiles:
+                transpose_x(i + 3)
+            if i in tiles:
+                k_mx[i] = quantise_row_tiles(k_grouped[i], k_mx_pool, "k")
+            if i + 2 in tiles:
+                x_mx[i + 2] = quantise_row_tiles(x_grouped[i + 2], x_mx_pool, "x")
+            if i + 1 in tiles:
+                project(i + 1, 0, 0)
+            for t in range(T):
+                if i + 1 in tiles:
+                    project(i + 1, 1 + 2 * t, 1 + t)
+                    project(i + 1, 2 + 2 * t, WE)
+                if i in tiles:
+                    fuse(i, t)
+
+        step(-3)
+        step(-2)
+        quantise_weights(w1_raw, w1_codes, w1_scales)
+        step(-1)
+        quantise_weights(w2_raw, w2_codes, w2_scales)
+        for i in range(E_TILES):
+            step(i)

@@ -32,6 +32,8 @@ def tile_comformerconvedgelayer_pa_t_kernel(
 ):
     nc = tc.nc
     with ExitStack() as stack:
+        stack.enter_context(tc.manual_schedule())
+
         def sbuf(name, bufs):
             return stack.enter_context(tc.tile_pool(name=name, bufs=bufs))
 

@@ -32,8 +32,6 @@ def tile_comformerconvedgelayer_pa_t_kernel(
 ):
     nc = tc.nc
     with ExitStack() as stack:
-        stack.enter_context(tc.manual_schedule())
-
         def sbuf(name, bufs):
             return stack.enter_context(tc.tile_pool(name=name, bufs=bufs))
 
@@ -79,11 +77,10 @@ def tile_comformerconvedgelayer_pa_t_kernel(
             nc.sync.dma_start(out=raw[:], in_=w.rearrange("(m p) c -> p m c", p=P))
             return raw
 
-        x_raw = [load_x(0), load_x(1)]
+        x_raw = [load_x(0)]
         w1_raw = [load_first_layer(w) for w in (Wk, Wke[0], Wke[1], Wke[2], We)]
-        x_raw.append(load_x(2))
         w2_raw = [load_second_layer(Wk1[g * C : (g + 1) * C, :]) for g in range(T)]
-        for i in range(3, E_TILES):
+        for i in range(1, E_TILES):
             x_raw.append(load_x(i))
 
         ident = const.tile([P, P], F32, name="ident")

@@ -46,6 +46,17 @@ def tile_comformerconvedgelayer_pa_t_kernel(
         hidden_pool = sbuf("hidden", 6)
         psum = stack.enter_context(tc.psum_pool(name="psum", bufs=PSUM_BANKS))
 
+        bias_rows = const.tile([P, P], BF16, name="bias_rows")
+        nc.vector.memset(bias_rows[:], 0.0)
+        ident = const.tile([P, P], F32, name="ident")
+        make_identity(nc, ident[:])
+        ident_bf16 = const.tile([P, P], BF16, name="ident_bf16")
+        nc.gpsimd.tensor_copy(out=ident_bf16[:], in_=ident[:])
+        ones = const.tile([P, P], BF16, name="ones")
+        nc.vector.memset(ones[:], 1.0)
+        bk1_row = const.tile([P, C], BF16, name="bk1_row")
+        nc.vector.memset(bk1_row[:], 0.0)
+
         def load_x(i):
             rows = slice(i * P, (i + 1) * P)
             raw = x_raw_pool.tile([P, ROW_TILES * C], BF16, name="x_raw")
@@ -77,94 +88,79 @@ def tile_comformerconvedgelayer_pa_t_kernel(
             nc.sync.dma_start(out=raw[:], in_=w.rearrange("(m p) c -> p m c", p=P))
             return raw
 
-        x_raw = [load_x(0)]
-        w1_raw = [load_first_layer(w) for w in (Wk, Wke[0], Wke[1], Wke[2], We)]
-        w2_raw = [load_second_layer(Wk1[g * C : (g + 1) * C, :]) for g in range(T)]
-        for i in range(1, E_TILES):
-            x_raw.append(load_x(i))
-
-        ident = const.tile([P, P], F32, name="ident")
-        make_identity(nc, ident[:])
-
-        bias_rows = const.tile([P, P], BF16, name="bias_rows")
-        nc.vector.memset(bias_rows[:], 0.0)
-        nc.scalar.dma_start(out=bias_rows[0:GROUPS, :], in_=bk.rearrange("(m p) -> m p", p=P))
-        nc.scalar.dma_start(
-            out=bias_rows[GROUPS : BIASED * GROUPS, :],
-            in_=bke.rearrange("t (m p) -> (t m) p", p=P),
-        )
-        bias_rows_f32 = const.tile([P, P], F32, name="bias_rows_f32")
-        nc.vector.tensor_copy(out=bias_rows_f32[:], in_=bias_rows[:])
-        bias_bank = psum.tile([P, P], F32, name="bias_bank", tag="bank")
-        nc.tensor.transpose(bias_bank[:], bias_rows_f32[:], ident[:])
-        bias1 = const.tile([P, BIASED * GROUPS], F32, name="bias1")
-        nc.vector.tensor_copy(out=bias1[:], in_=bias_bank[:, 0 : BIASED * GROUPS])
-
-        bk1_row = const.tile([P, C], BF16, name="bk1_row")
-        nc.vector.memset(bk1_row[:], 0.0)
-        nc.scalar.dma_start(out=bk1_row[0:1, :], in_=bk1.rearrange("(o c) -> o c", o=1))
-        ones = const.tile([P, P], BF16, name="ones")
-        nc.vector.memset(ones[:], 1.0)
-        bk1_bank = psum.tile([P, C], F32, name="bk1_bank", tag="bank")
-        nc.tensor.matmul(out=bk1_bank[:], lhsT=ones[:], rhs=bk1_row[:], start=True, stop=True)
-        bk1_all = const.tile([P, C], F32, name="bk1_all")
-        nc.vector.tensor_copy(out=bk1_all[:], in_=bk1_bank[:])
-
         w1_codes = const.tile([P, FIRST_LAYER * C], U32, name="w1_codes", align_bytes=64)
         w1_scales = const.tile([P, FIRST_LAYER * C], U8, name="w1_scales", align_bytes=64)
         w2_codes = const.tile([P, T * C], U32, name="w2_codes", align_bytes=64)
         w2_scales = const.tile([P, T * C], U8, name="w2_scales", align_bytes=64)
 
-        def quantise_weights(raws, codes, scales):
-            grouped = []
-            for n in range(len(raws) + 1):
-                if n < len(raws):
-                    tile = w_grouped_pool.tile([P, C, PACK], BF16, name="w_grouped", align_bytes=64)
-                    copy = nc.vector.tensor_copy if n % 2 == 0 else nc.scalar.copy
-                    copy(
-                        out=tile[:].rearrange("p (c i) j -> p c j i", i=4),
-                        in_=raws[n][:].rearrange("p j (c i) -> p c j i", i=4),
+        raw, x_raw, w_grouped = [], [], {}
+
+        def regroup_weight(w, copy):
+            tile = w_grouped_pool.tile([P, C, PACK], BF16, name="w_grouped", align_bytes=64)
+            half = C // 2
+            for h in range(2):
+                cols = slice(h * half, (h + 1) * half)
+                bank = psum.tile([P, PACK, half], BF16, name="w_bank", tag="bank")
+                for j in range(PACK):
+                    nc.tensor.matmul(
+                        out=bank[:, j, :],
+                        lhsT=ident_bf16[:],
+                        rhs=raw[w][:, j, cols],
+                        start=True,
+                        stop=True,
                     )
-                    grouped.append(tile)
-                if n > 0:
-                    cols = slice((n - 1) * C, n * C)
-                    nc.vector.quantize_mx(
-                        out=codes[:, cols].bitcast(FP8X4),
-                        scales=scales[:, cols],
-                        in_=grouped[n - 1][:].rearrange("p c j -> p (c j)"),
-                    )
+                copy(out=tile[:, cols, :], in_=bank[:].rearrange("p j c -> p c j"))
+            w_grouped[w] = tile
+
+        def quantise_weight(w):
+            first = w < FIRST_LAYER
+            codes, scales = (w1_codes, w1_scales) if first else (w2_codes, w2_scales)
+            place = w if first else w - FIRST_LAYER
+            cols = slice(place * C, (place + 1) * C)
+            nc.vector.quantize_mx(
+                out=codes[:, cols].bitcast(FP8X4),
+                scales=scales[:, cols],
+                in_=w_grouped[w][:].rearrange("p c j -> p (c j)"),
+            )
 
         x_grouped, x_mx, k_grouped, k_mx = {}, {}, {}, {}
+        stages = {"x": (x_grouped, x_mx, x_mx_pool), "k": (k_grouped, k_mx, k_mx_pool)}
 
-        def quantise_row_tiles(grouped, pool, name):
-            codes = pool.tile([P, ROW_TILES * P], U32, name=name + "_codes", align_bytes=64)
-            scales = pool.tile([P, ROW_TILES * P], U8, name=name + "_scales", align_bytes=64)
-            for first, count in UNITS:
-                words = slice(first * P, (first + count) * P)
-                nc.vector.quantize_mx(
-                    out=codes[:, words].bitcast(FP8X4),
-                    scales=scales[:, words],
-                    in_=grouped[:, first * C : (first + count) * C],
+        def quantise_unit(name, i, unit):
+            grouped, done, pool = stages[name]
+            if unit == 0:
+                done[i] = (
+                    pool.tile([P, ROW_TILES * P], U32, name=name + "_codes", align_bytes=64),
+                    pool.tile([P, ROW_TILES * P], U8, name=name + "_scales", align_bytes=64),
                 )
-            return codes, scales
+            codes, scales = done[i]
+            first, count = UNITS[unit]
+            words = slice(first * P, (first + count) * P)
+            nc.vector.quantize_mx(
+                out=codes[:, words].bitcast(FP8X4),
+                scales=scales[:, words],
+                in_=grouped[i][:, first * C : (first + count) * C],
+            )
 
-        def transpose_x(i):
-            grouped = x_grouped_pool.tile([P, ROW_TILES * C], BF16, name="x_grouped", align_bytes=64)
+        def transpose_unit(i, unit):
+            if unit == 0:
+                x_grouped[i] = x_grouped_pool.tile(
+                    [P, ROW_TILES * C], BF16, name="x_grouped", align_bytes=64
+                )
             words_in = x_raw[i][:].bitcast(F32)
-            words_out = grouped[:].bitcast(F32)
-            for first, count in UNITS:
-                bank = psum.tile([P, 2, 2, P], F32, name="xt", tag="bank")
-                for j in range(count):
-                    for u in range(2):
-                        word = place_in_x_raw(first + j) * WORDS + u * P
-                        nc.tensor.transpose(bank[:, j, u, :], words_in[:, word : word + P], ident[:])
-                nc.scalar.copy(
-                    out=words_out[:, first * WORDS : (first + count) * WORDS].rearrange(
-                        "p (j r u) -> p j r u", j=count, u=2
-                    ),
-                    in_=bank[:, 0:count].rearrange("p j u r -> p j r u"),
-                )
-            x_grouped[i] = grouped
+            words_out = x_grouped[i][:].bitcast(F32)
+            first, count = UNITS[unit]
+            bank = psum.tile([P, 2, 2, P], F32, name="xt", tag="bank")
+            for j in range(count):
+                for u in range(2):
+                    word = place_in_x_raw(first + j) * WORDS + u * P
+                    nc.tensor.transpose(bank[:, j, u, :], words_in[:, word : word + P], ident[:])
+            nc.scalar.copy(
+                out=words_out[:, first * WORDS : (first + count) * WORDS].rearrange(
+                    "p (j r u) -> p j r u", j=count, u=2
+                ),
+                in_=bank[:, 0:count].rearrange("p j u r -> p j r u"),
+            )
 
         def project(i, s, w):
             if s == 0:
@@ -213,27 +209,100 @@ def tile_comformerconvedgelayer_pa_t_kernel(
             nc.scalar.activation(out=hidden[:], in_=hidden[:], func=SILU)
             nc.sync.dma_start(out=out[i * P : (i + 1) * P, t, :], in_=hidden[:])
 
+        def load_all():
+            nc.sync.dma_start(out=bias_rows[0:GROUPS, :], in_=bk.rearrange("(m p) -> m p", p=P))
+            nc.sync.dma_start(
+                out=bias_rows[GROUPS : BIASED * GROUPS, :],
+                in_=bke.rearrange("t (m p) -> (t m) p", p=P),
+            )
+            raw.append(load_first_layer(Wk))
+            x_raw.append(load_x(0))
+            raw.extend(load_first_layer(w) for w in (Wke[0], Wke[1], Wke[2], We))
+            x_raw.append(load_x(1))
+            raw.extend(load_second_layer(Wk1[g * C : (g + 1) * C, :]) for g in range(T))
+            nc.sync.dma_start(out=bk1_row[0:1, :], in_=bk1.rearrange("(o c) -> o c", o=1))
+            for i in range(2, E_TILES):
+                x_raw.append(load_x(i))
+
+        bias1 = const.tile([P, BIASED * GROUPS], F32, name="bias1")
+
+        def spread_bias1():
+            bank = psum.tile([P, BIASED * GROUPS], F32, name="bias_bank", tag="bank")
+            nc.tensor.matmul(
+                out=bank[:],
+                lhsT=bias_rows[:],
+                rhs=ident_bf16[:, 0 : BIASED * GROUPS],
+                start=True,
+                stop=True,
+            )
+            nc.scalar.copy(out=bias1[:], in_=bank[:])
+
+        bk1_all = const.tile([P, C], F32, name="bk1_all")
+
+        def spread_bk1():
+            bank = psum.tile([P, C], F32, name="bk1_bank", tag="bank")
+            nc.tensor.matmul(out=bank[:], lhsT=ones[:], rhs=bk1_row[:], start=True, stop=True)
+            nc.scalar.copy(out=bk1_all[:], in_=bank[:])
+
+        on_vector, on_scalar = nc.vector.tensor_copy, nc.scalar.copy
+        units = range(len(UNITS))
+
         def step(i):
             tiles = range(E_TILES)
             if i + 3 in tiles:
-                transpose_x(i + 3)
+                for unit in units:
+                    transpose_unit(i + 3, unit)
             if i in tiles:
-                k_mx[i] = quantise_row_tiles(k_grouped[i], k_mx_pool, "k")
+                for unit in units:
+                    quantise_unit("k", i, unit)
             if i + 2 in tiles:
-                x_mx[i + 2] = quantise_row_tiles(x_grouped[i + 2], x_mx_pool, "x")
+                for unit in units:
+                    quantise_unit("x", i + 2, unit)
             if i + 1 in tiles:
                 project(i + 1, 0, 0)
             for t in range(T):
                 if i + 1 in tiles:
                     project(i + 1, 1 + 2 * t, 1 + t)
                     project(i + 1, 2 + 2 * t, WE)
-                if i in tiles:
+                if i == 0:
+                    regroup_weight(FIRST_LAYER + t, on_scalar)
+                    quantise_weight(FIRST_LAYER + t)
+                if i == 1:
+                    fuse(0, t)
+                if i > 0:
                     fuse(i, t)
 
-        step(-3)
-        step(-2)
-        quantise_weights(w1_raw, w1_codes, w1_scales)
-        step(-1)
-        quantise_weights(w2_raw, w2_codes, w2_scales)
-        for i in range(E_TILES):
-            step(i)
+        with tc.manual_schedule():
+            load_all()
+            regroup_weight(0, on_scalar)
+            transpose_unit(0, 0)
+            spread_bias1()
+            quantise_unit("x", 0, 0)
+            quantise_weight(0)
+            for unit in units[1:]:
+                transpose_unit(0, unit)
+            project(0, 0, 0)
+            for unit in units[1:]:
+                quantise_unit("x", 0, unit)
+            regroup_weight(1, on_scalar)
+            quantise_weight(1)
+            regroup_weight(2, on_scalar)
+            project(0, 1, 1)
+            quantise_weight(2)
+            regroup_weight(3, on_scalar)
+            project(0, 3, 2)
+            quantise_weight(3)
+            regroup_weight(4, on_scalar)
+            project(0, 5, 3)
+            quantise_weight(4)
+            for unit in units:
+                transpose_unit(1, unit)
+            for unit in units:
+                quantise_unit("x", 1, unit)
+            for s in (2, 4, 6):
+                project(0, s, WE)
+            for unit in units:
+                transpose_unit(2, unit)
+            spread_bk1()
+            for i in range(E_TILES):
+                step(i)

@@ -57,19 +57,25 @@ def tile_comformerconvedgelayer_pa_t_kernel(
         bk1_row = const.tile([P, C], BF16, name="bk1_row")
         nc.vector.memset(bk1_row[:], 0.0)
 
-        def load_x(i):
+        def load_edge(i):
+            tile = x_raw_pool.tile([P, ROW_TILES * C], BF16, name="x_raw")
+            nc.sync.dma_start(out=tile[:, 0:C], in_=edge[i * P : (i + 1) * P, :])
+            x_raw.append(tile)
+
+        def load_neighbours(i):
             rows = slice(i * P, (i + 1) * P)
-            raw = x_raw_pool.tile([P, ROW_TILES * C], BF16, name="x_raw")
-            nc.sync.dma_start(out=raw[:, 0:C], in_=edge[rows, :])
             nc.sync.dma_start(
-                out=raw[:, C : (1 + T) * C],
+                out=x_raw[i][:, C : (1 + T) * C],
                 in_=edge_nei_len[rows].rearrange("e t c -> e (t c)"),
             )
             nc.sync.dma_start(
-                out=raw[:, (1 + T) * C : ROW_TILES * C],
+                out=x_raw[i][:, (1 + T) * C : ROW_TILES * C],
                 in_=edge_nei_angle[rows].rearrange("e t c -> e (t c)"),
             )
-            return raw
+
+        def load_x(i):
+            load_edge(i)
+            load_neighbours(i)
 
         def place_in_x_raw(s):
             t, is_angle = divmod(s - 1, 2)
@@ -97,19 +103,10 @@ def tile_comformerconvedgelayer_pa_t_kernel(
 
         def regroup_weight(w, copy):
             tile = w_grouped_pool.tile([P, C, PACK], BF16, name="w_grouped", align_bytes=64)
-            half = C // 2
-            for h in range(2):
-                cols = slice(h * half, (h + 1) * half)
-                bank = psum.tile([P, PACK, half], BF16, name="w_bank", tag="bank")
-                for j in range(PACK):
-                    nc.tensor.matmul(
-                        out=bank[:, j, :],
-                        lhsT=ident_bf16[:],
-                        rhs=raw[w][:, j, cols],
-                        start=True,
-                        stop=True,
-                    )
-                copy(out=tile[:, cols, :], in_=bank[:].rearrange("p j c -> p c j"))
+            copy(
+                out=tile[:].rearrange("p (c i) j -> p c j i", i=4),
+                in_=raw[w][:].rearrange("p j (c i) -> p c j i", i=4),
+            )
             w_grouped[w] = tile
 
         def quantise_weight(w):
@@ -210,19 +207,20 @@ def tile_comformerconvedgelayer_pa_t_kernel(
             nc.sync.dma_start(out=out[i * P : (i + 1) * P, t, :], in_=hidden[:])
 
         def load_all():
+            raw.append(load_first_layer(Wk))
+            load_edge(0)
             nc.sync.dma_start(out=bias_rows[0:GROUPS, :], in_=bk.rearrange("(m p) -> m p", p=P))
             nc.sync.dma_start(
                 out=bias_rows[GROUPS : BIASED * GROUPS, :],
                 in_=bke.rearrange("t (m p) -> (t m) p", p=P),
             )
-            raw.append(load_first_layer(Wk))
-            x_raw.append(load_x(0))
+            load_neighbours(0)
             raw.extend(load_first_layer(w) for w in (Wke[0], Wke[1], Wke[2], We))
-            x_raw.append(load_x(1))
+            load_x(1)
             raw.extend(load_second_layer(Wk1[g * C : (g + 1) * C, :]) for g in range(T))
             nc.sync.dma_start(out=bk1_row[0:1, :], in_=bk1.rearrange("(o c) -> o c", o=1))
             for i in range(2, E_TILES):
-                x_raw.append(load_x(i))
+                load_x(i)
 
         bias1 = const.tile([P, BIASED * GROUPS], F32, name="bias1")
 
@@ -249,7 +247,7 @@ def tile_comformerconvedgelayer_pa_t_kernel(
 
         def step(i):
             tiles = range(E_TILES)
-            if i + 3 in tiles:
+            if i + 3 in tiles and i > 1:
                 for unit in units:
                     transpose_unit(i + 3, unit)
             if i in tiles:
@@ -258,51 +256,59 @@ def tile_comformerconvedgelayer_pa_t_kernel(
             if i + 2 in tiles:
                 for unit in units:
                     quantise_unit("x", i + 2, unit)
+            if i == 1:
+                regroup_weight(FIRST_LAYER + 2, on_vector)
             if i + 1 in tiles:
                 project(i + 1, 0, 0)
             for t in range(T):
                 if i + 1 in tiles:
                     project(i + 1, 1 + 2 * t, 1 + t)
                     project(i + 1, 2 + 2 * t, WE)
-                if i == 0:
-                    regroup_weight(FIRST_LAYER + t, on_scalar)
-                    quantise_weight(FIRST_LAYER + t)
                 if i == 1:
+                    quantise_weight(FIRST_LAYER + t)
+                if i == 2:
                     fuse(0, t)
-                if i > 0:
+                    fuse(1, t)
+                if i > 1:
                     fuse(i, t)
+            if i <= 1:
+                for unit in units:
+                    transpose_unit(i + 3, unit)
+            if i == 0:
+                regroup_weight(FIRST_LAYER, on_scalar)
+                regroup_weight(FIRST_LAYER + 1, on_scalar)
 
-        with tc.manual_schedule():
-            load_all()
-            regroup_weight(0, on_scalar)
-            transpose_unit(0, 0)
-            spread_bias1()
-            quantise_unit("x", 0, 0)
-            quantise_weight(0)
-            for unit in units[1:]:
-                transpose_unit(0, unit)
-            project(0, 0, 0)
-            for unit in units[1:]:
-                quantise_unit("x", 0, unit)
-            regroup_weight(1, on_scalar)
-            quantise_weight(1)
-            regroup_weight(2, on_scalar)
-            project(0, 1, 1)
-            quantise_weight(2)
-            regroup_weight(3, on_scalar)
-            project(0, 3, 2)
-            quantise_weight(3)
-            regroup_weight(4, on_scalar)
-            project(0, 5, 3)
-            quantise_weight(4)
-            for unit in units:
-                transpose_unit(1, unit)
-            for unit in units:
-                quantise_unit("x", 1, unit)
-            for s in (2, 4, 6):
-                project(0, s, WE)
-            for unit in units:
-                transpose_unit(2, unit)
-            spread_bk1()
-            for i in range(E_TILES):
-                step(i)
+        load_all()
+        regroup_weight(0, on_vector)
+        transpose_unit(0, 0)
+        spread_bias1()
+        quantise_unit("x", 0, 0)
+        quantise_weight(0)
+        for unit in units[1:]:
+            transpose_unit(0, unit)
+        quantise_unit("x", 0, 1)
+        regroup_weight(1, on_vector)
+        project(0, 0, 0)
+        regroup_weight(2, on_scalar)
+        quantise_unit("x", 0, 2)
+        quantise_weight(1)
+        quantise_unit("x", 0, 3)
+        regroup_weight(3, on_vector)
+        project(0, 1, 1)
+        quantise_weight(2)
+        regroup_weight(4, on_scalar)
+        quantise_weight(3)
+        project(0, 3, 2)
+        project(0, 5, 3)
+        for unit in units:
+            transpose_unit(1, unit)
+        quantise_weight(4)
+        for unit in units:
+            quantise_unit("x", 1, unit)
+        for s in (2, 4, 6):
+            project(0, s, WE)
+        for unit in units:
+            transpose_unit(2, unit)
+        spread_bk1()
+        for i in range(E_TILES):
+            step(i)

@@ -278,37 +278,38 @@ def tile_comformerconvedgelayer_pa_t_kernel(
                 regroup_weight(FIRST_LAYER, on_scalar)
                 regroup_weight(FIRST_LAYER + 1, on_scalar)
 
-        load_all()
-        regroup_weight(0, on_vector)
-        transpose_unit(0, 0)
-        spread_bias1()
-        quantise_unit("x", 0, 0)
-        quantise_weight(0)
-        for unit in units[1:]:
-            transpose_unit(0, unit)
-        quantise_unit("x", 0, 1)
-        regroup_weight(1, on_vector)
-        project(0, 0, 0)
-        regroup_weight(2, on_scalar)
-        quantise_unit("x", 0, 2)
-        quantise_weight(1)
-        quantise_unit("x", 0, 3)
-        regroup_weight(3, on_vector)
-        project(0, 1, 1)
-        quantise_weight(2)
-        regroup_weight(4, on_scalar)
-        quantise_weight(3)
-        project(0, 3, 2)
-        project(0, 5, 3)
-        for unit in units:
-            transpose_unit(1, unit)
-        quantise_weight(4)
-        for unit in units:
-            quantise_unit("x", 1, unit)
-        for s in (2, 4, 6):
-            project(0, s, WE)
-        for unit in units:
-            transpose_unit(2, unit)
-        spread_bk1()
-        for i in range(E_TILES):
-            step(i)
+        with tc.manual_schedule(engines={mybir.EngineType.PE}):
+            load_all()
+            regroup_weight(0, on_vector)
+            transpose_unit(0, 0)
+            spread_bias1()
+            quantise_unit("x", 0, 0)
+            quantise_weight(0)
+            for unit in units[1:]:
+                transpose_unit(0, unit)
+            quantise_unit("x", 0, 1)
+            regroup_weight(1, on_vector)
+            project(0, 0, 0)
+            regroup_weight(2, on_scalar)
+            quantise_unit("x", 0, 2)
+            quantise_weight(1)
+            quantise_unit("x", 0, 3)
+            regroup_weight(3, on_vector)
+            project(0, 1, 1)
+            quantise_weight(2)
+            regroup_weight(4, on_scalar)
+            quantise_weight(3)
+            project(0, 3, 2)
+            project(0, 5, 3)
+            for unit in units:
+                transpose_unit(1, unit)
+            quantise_weight(4)
+            for unit in units:
+                quantise_unit("x", 1, unit)
+            for s in (2, 4, 6):
+                project(0, s, WE)
+            for unit in units:
+                transpose_unit(2, unit)
+            spread_bk1()
+            for i in range(E_TILES):
+                step(i)

@@ -81,12 +81,21 @@ def tile_comformerconvedgelayer_pa_t_kernel(
             t, is_angle = divmod(s - 1, 2)
             return 0 if s == 0 else 1 + T * is_angle + t
 
-        def load_first_layer(w):
+        def load_first_layer(w, pieces=1):
             raw = w_raw_pool.tile([P, PACK, C], BF16, name="w_raw")
-            nc.sync.dma_start(
-                out=raw[:].rearrange("p (u e) c -> p u (e c)", u=2),
-                in_=w.rearrange("(u p e) c -> p u (e c)", u=2, e=2),
-            )
+            if pieces == 1:
+                nc.sync.dma_start(
+                    out=raw[:].rearrange("p (u e) c -> p u (e c)", u=2),
+                    in_=w.rearrange("(u p e) c -> p u (e c)", u=2, e=2),
+                )
+                return raw
+            for piece in range(pieces):
+                cols = slice(piece * C // pieces, (piece + 1) * C // pieces)
+                for u in range(2):
+                    nc.sync.dma_start(
+                        out=raw[:, 2 * u : 2 * u + 2, cols],
+                        in_=w[u * 2 * P : (u + 1) * 2 * P, cols].rearrange("(p e) c -> p e c", e=2),
+                    )
             return raw
 
         def load_second_layer(w):
@@ -101,12 +110,14 @@ def tile_comformerconvedgelayer_pa_t_kernel(
 
         raw, x_raw, w_grouped = [], [], {}
 
-        def regroup_weight(w, copy):
+        def regroup_weight(w, copy, pieces=1):
             tile = w_grouped_pool.tile([P, C, PACK], BF16, name="w_grouped", align_bytes=64)
-            copy(
-                out=tile[:].rearrange("p (c i) j -> p c j i", i=4),
-                in_=raw[w][:].rearrange("p j (c i) -> p c j i", i=4),
-            )
+            for piece in range(pieces):
+                cols = slice(piece * C // pieces, (piece + 1) * C // pieces)
+                copy(
+                    out=tile[:, cols, :].rearrange("p (c i) j -> p c j i", i=4),
+                    in_=raw[w][:, :, cols].rearrange("p j (c i) -> p c j i", i=4),
+                )
             w_grouped[w] = tile
 
         def quantise_weight(w):
@@ -125,13 +136,15 @@ def tile_comformerconvedgelayer_pa_t_kernel(
 
         def quantise_unit(name, i, unit):
             grouped, done, pool = stages[name]
+            if unit == 1:
+                return
             if unit == 0:
                 done[i] = (
                     pool.tile([P, ROW_TILES * P], U32, name=name + "_codes", align_bytes=64),
                     pool.tile([P, ROW_TILES * P], U8, name=name + "_scales", align_bytes=64),
                 )
             codes, scales = done[i]
-            first, count = UNITS[unit]
+            first, count = UNITS[unit] if unit != 2 else (1, 4)
             words = slice(first * P, (first + count) * P)
             nc.vector.quantize_mx(
                 out=codes[:, words].bitcast(FP8X4),
@@ -188,38 +201,43 @@ def tile_comformerconvedgelayer_pa_t_kernel(
 
         def fuse(i, t):
             codes, scales = k_mx[i]
-            acc = psum.tile([P, C], F32, name="acc", tag="bank")
-            for g, s in enumerate((0, 1 + 2 * t, 2 + 2 * t)):
-                rows = slice(s * P, (s + 1) * P)
-                w_cols = slice(g * C, (g + 1) * C)
-                nc.tensor.matmul_mx(
-                    out=acc[:],
-                    lhsT=codes[:, rows].bitcast(FP8X4),
-                    lhsT_scale=scales[:, rows],
-                    rhs=w2_codes[:, w_cols].bitcast(FP8X4),
-                    rhs_scale=w2_scales[:, w_cols],
-                    start=(g == 0),
-                    stop=(g == 2),
-                )
-            hidden = hidden_pool.tile([P, C], F32, name="hidden")
-            nc.vector.tensor_tensor(out=hidden[:], in0=acc[:], in1=bk1_all[:], op=ADD)
-            nc.scalar.activation(out=hidden[:], in_=hidden[:], func=SILU)
-            nc.sync.dma_start(out=out[i * P : (i + 1) * P, t, :], in_=hidden[:])
+            pieces = 2 if (i, t) == (E_TILES - 1, T - 1) else 1
+            width = C // pieces
+            for piece in range(pieces):
+                acc = psum.tile([P, width], F32, name="acc", tag="bank")
+                for g, s in enumerate((0, 1 + 2 * t, 2 + 2 * t)):
+                    rows = slice(s * P, (s + 1) * P)
+                    first = g * C + piece * width
+                    w_cols = slice(first, first + width)
+                    nc.tensor.matmul_mx(
+                        out=acc[:],
+                        lhsT=codes[:, rows].bitcast(FP8X4),
+                        lhsT_scale=scales[:, rows],
+                        rhs=w2_codes[:, w_cols].bitcast(FP8X4),
+                        rhs_scale=w2_scales[:, w_cols],
+                        start=(g == 0),
+                        stop=(g == 2),
+                    )
+                cols = slice(piece * width, (piece + 1) * width)
+                hidden = hidden_pool.tile([P, width], F32, name="hidden")
+                nc.vector.tensor_tensor(out=hidden[:], in0=acc[:], in1=bk1_all[:, cols], op=ADD)
+                nc.scalar.activation(out=hidden[:], in_=hidden[:], func=SILU)
+                nc.sync.dma_start(out=out[i * P : (i + 1) * P, t, cols], in_=hidden[:])
 
         def load_all():
-            raw.append(load_first_layer(Wk))
+            raw.append(load_first_layer(Wk, pieces=2))
             load_edge(0)
             nc.sync.dma_start(out=bias_rows[0:GROUPS, :], in_=bk.rearrange("(m p) -> m p", p=P))
             nc.sync.dma_start(
                 out=bias_rows[GROUPS : BIASED * GROUPS, :],
                 in_=bke.rearrange("t (m p) -> (t m) p", p=P),
             )
+            raw.append(load_first_layer(Wke[0]))
             load_neighbours(0)
-            raw.extend(load_first_layer(w) for w in (Wke[0], Wke[1], Wke[2], We))
-            load_x(1)
+            raw.extend(load_first_layer(w) for w in (Wke[1], Wke[2], We))
             raw.extend(load_second_layer(Wk1[g * C : (g + 1) * C, :]) for g in range(T))
             nc.sync.dma_start(out=bk1_row[0:1, :], in_=bk1.rearrange("(o c) -> o c", o=1))
-            for i in range(2, E_TILES):
+            for i in range(1, E_TILES):
                 load_x(i)
 
         bias1 = const.tile([P, BIASED * GROUPS], F32, name="bias1")
@@ -253,6 +271,8 @@ def tile_comformerconvedgelayer_pa_t_kernel(
             if i in tiles:
                 for unit in units:
                     quantise_unit("k", i, unit)
+                    if i == E_TILES - 1 and unit > 0:
+                        fuse(i - 1, unit - 1)
             if i + 2 in tiles:
                 for unit in units:
                     quantise_unit("x", i + 2, unit)
@@ -268,28 +288,29 @@ def tile_comformerconvedgelayer_pa_t_kernel(
                     quantise_weight(FIRST_LAYER + t)
                 if i == 2:
                     fuse(0, t)
-                    fuse(1, t)
-                if i > 1:
+                if 1 < i < E_TILES - 1:
+                    fuse(i - 1, t)
+                if i == E_TILES - 1:
                     fuse(i, t)
             if i <= 1:
                 for unit in units:
                     transpose_unit(i + 3, unit)
             if i == 0:
-                regroup_weight(FIRST_LAYER, on_scalar)
+                regroup_weight(FIRST_LAYER, on_vector)
                 regroup_weight(FIRST_LAYER + 1, on_scalar)
 
-        with tc.manual_schedule(engines={mybir.EngineType.PE}):
+        with tc.manual_schedule(engines={mybir.EngineType.PE, mybir.EngineType.SP}):
             load_all()
-            regroup_weight(0, on_vector)
+            regroup_weight(0, on_vector, pieces=2)
             transpose_unit(0, 0)
             spread_bias1()
             quantise_unit("x", 0, 0)
             quantise_weight(0)
+            project(0, 0, 0)
             for unit in units[1:]:
                 transpose_unit(0, unit)
             quantise_unit("x", 0, 1)
             regroup_weight(1, on_vector)
-            project(0, 0, 0)
             regroup_weight(2, on_scalar)
             quantise_unit("x", 0, 2)
             quantise_weight(1)

@@ -36,14 +36,14 @@ def tile_comformerconvedgelayer_pa_t_kernel(
             return stack.enter_context(tc.tile_pool(name=name, bufs=bufs))
 
         const = sbuf("const", 1)
-        x_raw_pool = sbuf("x_raw", E_TILES)
+        x_raw_pool = sbuf("x_raw", 9)
         w_raw_pool = sbuf("w_raw", FIRST_LAYER + T)
         w_grouped_pool = sbuf("w_grouped", 3)
-        x_grouped_pool = sbuf("x_grouped", 3)
+        x_grouped_pool = sbuf("x_grouped", 4)
         x_mx_pool = sbuf("x_mx", 3)
-        k_grouped_pool = sbuf("k_grouped", 3)
+        k_grouped_pool = sbuf("k_grouped", 4)
         k_mx_pool = sbuf("k_mx", 3)
-        hidden_pool = sbuf("hidden", 6)
+        hidden_pool = sbuf("hidden", 8)
         psum = stack.enter_context(tc.psum_pool(name="psum", bufs=PSUM_BANKS))
 
         bias_rows = const.tile([P, P], BF16, name="bias_rows")
@@ -277,7 +277,7 @@ def tile_comformerconvedgelayer_pa_t_kernel(
                 for unit in units:
                     quantise_unit("x", i + 2, unit)
             if i == 1:
-                regroup_weight(FIRST_LAYER + 2, on_vector)
+                regroup_weight(FIRST_LAYER + 2, on_vector, pieces=2)
             if i + 1 in tiles:
                 project(i + 1, 0, 0)
             for t in range(T):
@@ -296,8 +296,8 @@ def tile_comformerconvedgelayer_pa_t_kernel(
                 for unit in units:
                     transpose_unit(i + 3, unit)
             if i == 0:
-                regroup_weight(FIRST_LAYER, on_vector)
-                regroup_weight(FIRST_LAYER + 1, on_scalar)
+                regroup_weight(FIRST_LAYER, on_vector, pieces=2)
+                regroup_weight(FIRST_LAYER + 1, on_scalar, pieces=4)
 
         with tc.manual_schedule(engines={mybir.EngineType.PE, mybir.EngineType.SP}):
             load_all()
@@ -311,14 +311,14 @@ def tile_comformerconvedgelayer_pa_t_kernel(
                 transpose_unit(0, unit)
             quantise_unit("x", 0, 1)
             regroup_weight(1, on_vector)
-            regroup_weight(2, on_scalar)
+            regroup_weight(2, on_scalar, pieces=4)
             quantise_unit("x", 0, 2)
             quantise_weight(1)
             quantise_unit("x", 0, 3)
             regroup_weight(3, on_vector)
             project(0, 1, 1)
             quantise_weight(2)
-            regroup_weight(4, on_scalar)
+            regroup_weight(4, on_scalar, pieces=4)
             quantise_weight(3)
             project(0, 3, 2)
             project(0, 5, 3)

@@ -36,10 +36,10 @@ def tile_comformerconvedgelayer_pa_t_kernel(
             return stack.enter_context(tc.tile_pool(name=name, bufs=bufs))
 
         const = sbuf("const", 1)
-        x_raw_pool = sbuf("x_raw", 9)
+        x_raw_pool = sbuf("x_raw", E_TILES)
         w_raw_pool = sbuf("w_raw", FIRST_LAYER + T)
         w_grouped_pool = sbuf("w_grouped", 3)
-        x_grouped_pool = sbuf("x_grouped", 4)
+        x_grouped_pool = sbuf("x_grouped", 3)
         x_mx_pool = sbuf("x_mx", 3)
         k_grouped_pool = sbuf("k_grouped", 4)
         k_mx_pool = sbuf("k_mx", 3)

from contextlib import ExitStack

import concourse.mybir as mybir
from concourse.masks import make_identity

F32 = mybir.dt.float32
BF16 = mybir.dt.bfloat16
U32 = mybir.dt.uint32
U8 = mybir.dt.uint8
FP8X4 = mybir.dt.float8_e4m3fn_x4
ADD = mybir.AluOpType.add
SILU = mybir.ActivationFunctionType.Silu

P = 128
PACK = 4
E, T, C = 1408, 3, 512
E_TILES = E // P
ROW_TILES = 1 + 2 * T
GROUPS = C // P
WORDS = C // 2
PSUM_BANKS = 8
FIRST_LAYER = 2 + T
BIASED = 1 + T
WE = 1 + T
UNITS = ((0, 1), (1, 2), (3, 2), (5, 2))

FLOPS = 2 * 2 * ROW_TILES * E * C * C


def tile_comformerconvedgelayer_pa_t_kernel(
    tc, edge, edge_nei_len, edge_nei_angle, Wk, bk, Wke, bke, We, Wk1, bk1, out
):
    nc = tc.nc
    with ExitStack() as stack:
        def sbuf(name, bufs):
            return stack.enter_context(tc.tile_pool(name=name, bufs=bufs))

        const = sbuf("const", 1)
        x_raw_pool = sbuf("x_raw", E_TILES)
        w_raw_pool = sbuf("w_raw", FIRST_LAYER + T)
        w_grouped_pool = sbuf("w_grouped", 3)
        x_grouped_pool = sbuf("x_grouped", 3)
        x_mx_pool = sbuf("x_mx", 3)
        k_grouped_pool = sbuf("k_grouped", 4)
        k_mx_pool = sbuf("k_mx", 3)
        hidden_pool = sbuf("hidden", 8)
        psum = stack.enter_context(tc.psum_pool(name="psum", bufs=PSUM_BANKS))

        bias_rows = const.tile([P, P], BF16, name="bias_rows")
        nc.vector.memset(bias_rows[:], 0.0)
        ident = const.tile([P, P], F32, name="ident")
        make_identity(nc, ident[:])
        ident_bf16 = const.tile([P, P], BF16, name="ident_bf16")
        nc.gpsimd.tensor_copy(out=ident_bf16[:], in_=ident[:])
        ones = const.tile([P, P], BF16, name="ones")
        nc.vector.memset(ones[:], 1.0)
        bk1_row = const.tile([P, C], BF16, name="bk1_row")
        nc.vector.memset(bk1_row[:], 0.0)

        def load_edge(i):
            tile = x_raw_pool.tile([P, ROW_TILES * C], BF16, name="x_raw")
            nc.sync.dma_start(out=tile[:, 0:C], in_=edge[i * P : (i + 1) * P, :])
            x_raw.append(tile)

        def load_neighbours(i):
            rows = slice(i * P, (i + 1) * P)
            nc.sync.dma_start(
                out=x_raw[i][:, C : (1 + T) * C],
                in_=edge_nei_len[rows].rearrange("e t c -> e (t c)"),
            )
            nc.sync.dma_start(
                out=x_raw[i][:, (1 + T) * C : ROW_TILES * C],
                in_=edge_nei_angle[rows].rearrange("e t c -> e (t c)"),
            )

        def load_x(i):
            load_edge(i)
            load_neighbours(i)

        def place_in_x_raw(s):
            t, is_angle = divmod(s - 1, 2)
            return 0 if s == 0 else 1 + T * is_angle + t

        def load_first_layer(w, pieces=1):
            raw = w_raw_pool.tile([P, PACK, C], BF16, name="w_raw")
            if pieces == 1:
                nc.sync.dma_start(
                    out=raw[:].rearrange("p (u e) c -> p u (e c)", u=2),
                    in_=w.rearrange("(u p e) c -> p u (e c)", u=2, e=2),
                )
                return raw
            for piece in range(pieces):
                cols = slice(piece * C // pieces, (piece + 1) * C // pieces)
                for u in range(2):
                    nc.sync.dma_start(
                        out=raw[:, 2 * u : 2 * u + 2, cols],
                        in_=w[u * 2 * P : (u + 1) * 2 * P, cols].rearrange("(p e) c -> p e c", e=2),
                    )
            return raw

        def load_second_layer(w):
            raw = w_raw_pool.tile([P, PACK, C], BF16, name="w_raw")
            nc.sync.dma_start(out=raw[:], in_=w.rearrange("(m p) c -> p m c", p=P))
            return raw

        w1_codes = const.tile([P, FIRST_LAYER * C], U32, name="w1_codes", align_bytes=64)
        w1_scales = const.tile([P, FIRST_LAYER * C], U8, name="w1_scales", align_bytes=64)
        w2_codes = const.tile([P, T * C], U32, name="w2_codes", align_bytes=64)
        w2_scales = const.tile([P, T * C], U8, name="w2_scales", align_bytes=64)

        raw, x_raw, w_grouped = [], [], {}

        def regroup_weight(w, copy, pieces=1):
            tile = w_grouped_pool.tile([P, C, PACK], BF16, name="w_grouped", align_bytes=64)
            for piece in range(pieces):
                cols = slice(piece * C // pieces, (piece + 1) * C // pieces)
                copy(
                    out=tile[:, cols, :].rearrange("p (c i) j -> p c j i", i=4),
                    in_=raw[w][:, :, cols].rearrange("p j (c i) -> p c j i", i=4),
                )
            w_grouped[w] = tile

        def quantise_weight(w):
            first = w < FIRST_LAYER
            codes, scales = (w1_codes, w1_scales) if first else (w2_codes, w2_scales)
            place = w if first else w - FIRST_LAYER
            cols = slice(place * C, (place + 1) * C)
            nc.vector.quantize_mx(
                out=codes[:, cols].bitcast(FP8X4),
                scales=scales[:, cols],
                in_=w_grouped[w][:].rearrange("p c j -> p (c j)"),
            )

        x_grouped, x_mx, k_grouped, k_mx = {}, {}, {}, {}
        stages = {"x": (x_grouped, x_mx, x_mx_pool), "k": (k_grouped, k_mx, k_mx_pool)}

        def quantise_unit(name, i, unit):
            grouped, done, pool = stages[name]
            if unit == 1:
                return
            if unit == 0:
                done[i] = (
                    pool.tile([P, ROW_TILES * P], U32, name=name + "_codes", align_bytes=64),
                    pool.tile([P, ROW_TILES * P], U8, name=name + "_scales", align_bytes=64),
                )
            codes, scales = done[i]
            first, count = UNITS[unit] if unit != 2 else (1, 4)
            words = slice(first * P, (first + count) * P)
            nc.vector.quantize_mx(
                out=codes[:, words].bitcast(FP8X4),
                scales=scales[:, words],
                in_=grouped[i][:, first * C : (first + count) * C],
            )

        def transpose_unit(i, unit):
            if unit == 0:
                x_grouped[i] = x_grouped_pool.tile(
                    [P, ROW_TILES * C], BF16, name="x_grouped", align_bytes=64
                )
            words_in = x_raw[i][:].bitcast(F32)
            words_out = x_grouped[i][:].bitcast(F32)
            first, count = UNITS[unit]
            bank = psum.tile([P, 2, 2, P], F32, name="xt", tag="bank")
            for j in range(count):
                for u in range(2):
                    word = place_in_x_raw(first + j) * WORDS + u * P
                    nc.tensor.transpose(bank[:, j, u, :], words_in[:, word : word + P], ident[:])
            nc.scalar.copy(
                out=words_out[:, first * WORDS : (first + count) * WORDS].rearrange(
                    "p (j r u) -> p j r u", j=count, u=2
                ),
                in_=bank[:, 0:count].rearrange("p j u r -> p j r u"),
            )

        def project(i, s, w):
            if s == 0:
                k_grouped[i] = k_grouped_pool.tile(
                    [P, ROW_TILES * C], BF16, name="k_grouped", align_bytes=64
                )
            codes, scales = x_mx[i]
            rows = slice(s * P, (s + 1) * P)
            bank = psum.tile([P, GROUPS, P], F32, name="k_bank", tag="bank")
            for m in range(GROUPS):
                channels = slice(w * C + m * P, w * C + (m + 1) * P)
                nc.tensor.matmul_mx(
                    out=bank[:, m, :],
                    lhsT=w1_codes[:, channels].bitcast(FP8X4),
                    lhsT_scale=w1_scales[:, channels],
                    rhs=codes[:, rows].bitcast(FP8X4),
                    rhs_scale=scales[:, rows],
                    start=True,
                    stop=True,
                )
            result = bank[:].rearrange("p m r -> p r m")
            rounded = k_grouped[i][:, s * C : (s + 1) * C].rearrange("p (r m) -> p r m", m=GROUPS)
            if w < BIASED:
                bias = bias1[:, w * GROUPS : (w + 1) * GROUPS].unsqueeze(1).to_broadcast([P, P, GROUPS])
                nc.vector.tensor_tensor(out=rounded, in0=result, in1=bias, op=ADD)
            else:
                nc.scalar.copy(out=rounded, in_=result)

        def fuse(i, t):
            codes, scales = k_mx[i]
            pieces = 2 if (i, t) == (E_TILES - 1, T - 1) else 1
            width = C // pieces
            for piece in range(pieces):
                acc = psum.tile([P, width], F32, name="acc", tag="bank")
                for g, s in enumerate((0, 1 + 2 * t, 2 + 2 * t)):
                    rows = slice(s * P, (s + 1) * P)
                    first = g * C + piece * width
                    w_cols = slice(first, first + width)
                    nc.tensor.matmul_mx(
                        out=acc[:],
                        lhsT=codes[:, rows].bitcast(FP8X4),
                        lhsT_scale=scales[:, rows],
                        rhs=w2_codes[:, w_cols].bitcast(FP8X4),
                        rhs_scale=w2_scales[:, w_cols],
                        start=(g == 0),
                        stop=(g == 2),
                    )
                cols = slice(piece * width, (piece + 1) * width)
                hidden = hidden_pool.tile([P, width], F32, name="hidden")
                nc.vector.tensor_tensor(out=hidden[:], in0=acc[:], in1=bk1_all[:, cols], op=ADD)
                nc.scalar.activation(out=hidden[:], in_=hidden[:], func=SILU)
                nc.sync.dma_start(out=out[i * P : (i + 1) * P, t, cols], in_=hidden[:])

        def load_all():
            raw.append(load_first_layer(Wk, pieces=2))
            load_edge(0)
            nc.sync.dma_start(out=bias_rows[0:GROUPS, :], in_=bk.rearrange("(m p) -> m p", p=P))
            nc.sync.dma_start(
                out=bias_rows[GROUPS : BIASED * GROUPS, :],
                in_=bke.rearrange("t (m p) -> (t m) p", p=P),
            )
            raw.append(load_first_layer(Wke[0]))
            load_neighbours(0)
            raw.extend(load_first_layer(w) for w in (Wke[1], Wke[2], We))
            raw.extend(load_second_layer(Wk1[g * C : (g + 1) * C, :]) for g in range(T))
            nc.sync.dma_start(out=bk1_row[0:1, :], in_=bk1.rearrange("(o c) -> o c", o=1))
            for i in range(1, E_TILES):
                load_x(i)

        bias1 = const.tile([P, BIASED * GROUPS], F32, name="bias1")

        def spread_bias1():
            bank = psum.tile([P, BIASED * GROUPS], F32, name="bias_bank", tag="bank")
            nc.tensor.matmul(
                out=bank[:],
                lhsT=bias_rows[:],
                rhs=ident_bf16[:, 0 : BIASED * GROUPS],
                start=True,
                stop=True,
            )
            nc.scalar.copy(out=bias1[:], in_=bank[:])

        bk1_all = const.tile([P, C], F32, name="bk1_all")

        def spread_bk1():
            bank = psum.tile([P, C], F32, name="bk1_bank", tag="bank")
            nc.tensor.matmul(out=bank[:], lhsT=ones[:], rhs=bk1_row[:], start=True, stop=True)
            nc.scalar.copy(out=bk1_all[:], in_=bank[:])

        on_vector, on_scalar = nc.vector.tensor_copy, nc.scalar.copy
        units = range(len(UNITS))

        def step(i):
            tiles = range(E_TILES)
            if i + 3 in tiles and i > 1:
                for unit in units:
                    transpose_unit(i + 3, unit)
            if i in tiles:
                for unit in units:
                    quantise_unit("k", i, unit)
                    if i == E_TILES - 1 and unit > 0:
                        fuse(i - 1, unit - 1)
            if i + 2 in tiles:
                for unit in units:
                    quantise_unit("x", i + 2, unit)
            if i == 1:
                regroup_weight(FIRST_LAYER + 2, on_vector, pieces=2)
            if i + 1 in tiles:
                project(i + 1, 0, 0)
            for t in range(T):
                if i + 1 in tiles:
                    project(i + 1, 1 + 2 * t, 1 + t)
                    project(i + 1, 2 + 2 * t, WE)
                if i == 1:
                    quantise_weight(FIRST_LAYER + t)
                if i == 2:
                    fuse(0, t)
                if 1 < i < E_TILES - 1:
                    fuse(i - 1, t)
                if i == E_TILES - 1:
                    fuse(i, t)
            if i <= 1:
                for unit in units:
                    transpose_unit(i + 3, unit)
            if i == 0:
                regroup_weight(FIRST_LAYER, on_vector, pieces=2)
                regroup_weight(FIRST_LAYER + 1, on_scalar, pieces=4)

        with tc.manual_schedule(engines={mybir.EngineType.PE, mybir.EngineType.SP}):
            load_all()
            regroup_weight(0, on_vector, pieces=2)
            transpose_unit(0, 0)
            spread_bias1()
            quantise_unit("x", 0, 0)
            quantise_weight(0)
            project(0, 0, 0)
            for unit in units[1:]:
                transpose_unit(0, unit)
            quantise_unit("x", 0, 1)
            regroup_weight(1, on_vector)
            regroup_weight(2, on_scalar, pieces=4)
            quantise_unit("x", 0, 2)
            quantise_weight(1)
            quantise_unit("x", 0, 3)
            regroup_weight(3, on_vector)
            project(0, 1, 1)
            quantise_weight(2)
            regroup_weight(4, on_scalar, pieces=4)
            quantise_weight(3)
            project(0, 3, 2)
            project(0, 5, 3)
            for unit in units:
                transpose_unit(1, unit)
            quantise_weight(4)
            for unit in units:
                quantise_unit("x", 1, unit)
            for s in (2, 4, 6):
                project(0, s, WE)
            for unit in units:
                transpose_unit(2, unit)
            spread_bk1()
            for i in range(E_TILES):
                step(i)
